import numpy as np
import ml_dtypes


BF16 = ml_dtypes.bfloat16


def bf(x):
    return np.asarray(x, np.float32).astype(BF16)


def f64(x):
    return np.asarray(x).astype(np.float64)


E2M1 = np.array([0.0, 0.5, 1.0, 1.5, 2.0, 3.0, 4.0, 6.0, -0.0, -0.5, -1.0, -1.5, -2.0, -3.0, -4.0, -6.0])


def pack_weight(w, fmt):
    k, n = w.shape
    w = f64(bf(w)).reshape(k // 32, 32, n)
    amax = np.abs(w).max(1)
    if fmt == "e4m3":
        byte = np.frexp(amax)[1] - 1 + 127 - 7
    else:
        mant, ex = np.frexp(amax / 6.0)
        byte = np.where(mant > 0.5, ex, ex - 1) + 127
    byte = np.clip(np.where(amax > 0, byte, 1), 1, 254)
    scaled = (w * np.exp2(127.0 - byte)[:, None, :]).reshape(k, n).astype(np.float32)
    by_word = np.ascontiguousarray(scaled.reshape(k // 512, 128, 4, n).transpose(0, 1, 3, 2))
    if fmt == "e4m3":
        words = by_word.astype(ml_dtypes.float8_e4m3fn).view(np.uint8)
    else:
        c = by_word.astype(ml_dtypes.float4_e2m1fn).view(np.uint8) & 0xF
        words = c[..., 0::2] | (c[..., 1::2] << 4)
    return np.ascontiguousarray(words), np.ascontiguousarray(byte.astype(np.uint8).reshape(k // 512, 16, n))


def unpack_weight(words, scales, fmt):
    g, p, n, _ = words.shape
    if fmt == "e4m3":
        vals = np.ascontiguousarray(words).view(ml_dtypes.float8_e4m3fn).astype(np.float64)
    else:
        nib = np.empty((g, p, n, 4), np.uint8)
        nib[..., 0::2] = words & 0xF
        nib[..., 1::2] = words >> 4
        vals = E2M1[nib]
    vals = vals * np.repeat(np.exp2(scales.astype(np.float64) - 127.0), 8, axis=1)[..., None]
    return vals.transpose(0, 1, 3, 2).reshape(g * 512, n)

def pack4(w):
    words, scales = pack_weight(w, "e2m1")
    return words.reshape(words.shape[0], 128, -1), scales


def unpack4(words, scales):
    return unpack_weight(words.reshape(words.shape[0], 128, -1, 2), scales, "e2m1")


def kspread(k):
    return np.exp2(np.repeat(np.random.randint(-6, 7, k // 32), 32).astype(np.float64))


T, DIM, H, HKV, D = 4096, 2048, 16, 4, 128
THETA = 10000.0
NQ, NK = H * D, HKV * D


def rope(u):
    inv_freq = 1.0 / THETA ** (np.arange(0, D, 2) / D)
    ang = np.arange(T)[:, None] * inv_freq
    cos, sin = np.cos(ang)[:, None, :], np.sin(ang)[:, None, :]
    p = u.reshape(T, -1, D // 2, 2)
    u1, u2 = p[..., 0], p[..., 1]
    return np.stack([u1 * cos - u2 * sin, u1 * sin + u2 * cos], axis=-1).reshape(u.shape)


def setup_inputs():
    s = kspread(DIM)
    x = np.random.standard_normal((T, DIM)) * s
    x_words, x_scales = pack4(x.reshape(T, DIM).T)
    words, scales = pack4((np.random.standard_normal((NQ + NK + NK, DIM)) / np.sqrt(DIM) / s).T)
    return {"x_words": x_words, "x_scales": x_scales, "w_qkv_words": words, "w_qkv_scales": scales}


def reference(x_words, x_scales, w_qkv_words, w_qkv_scales):
    qkv = unpack4(x_words, x_scales).T @ unpack4(w_qkv_words, w_qkv_scales)
    q = qkv[:, :NQ].reshape(T, H, D)
    k = qkv[:, NQ:NQ + NK].reshape(T, HKV, D)
    v = qkv[:, NQ + NK:].reshape(T, HKV, D)
    return rope(q), rope(k), v

@@ -1,0 +1,280 @@
+import math
+from contextlib import ExitStack
+
+import concourse.mybir as mybir
+
+T, DIM, H, HKV, D = 4096, 2048, 16, 4, 128
+THETA = 10000.0
+N_OUT = (H + 2 * HKV) * D
+FLOPS = 2 * T * DIM * N_OUT
+
+F32 = mybir.dt.float32
+I32 = mybir.dt.int32
+U8 = mybir.dt.uint8
+BF16 = mybir.dt.bfloat16
+FP4X4 = mybir.dt.float4_e2m1fn_x4
+ACT = mybir.ActivationFunctionType
+ALU = mybir.AluOpType
+
+P = 128
+PASSES = DIM // 512
+N_TILES = T // P
+NB = N_OUT // 512
+ROPE_BLOCKS = 5
+V_BLOCK = 5
+HALF = D // 2
+HEADS_PER_BLOCK = 512 // D
+GROUP = 4
+HEAD_TILES = 4
+DEFER_V = 8
+WARM_MATMULS = 12
+
+W_SCALE_GROUPS = ((5, 6), (0, 2), (2, 5))
+X_SCALE_GROUPS = ((0, 8), (8, 32))
+X_CODE_GROUPS = ((0, 2), (2, 4), (4, 8), (8, 16), (16, 24), (24, 32))
+
+TWO_PI_HI = 6.28125
+TWO_PI_LO = 2.0 * math.pi - TWO_PI_HI
+
+
+def find_group(groups, i):
+    for n, (lo, hi) in enumerate(groups):
+        if lo <= i < hi:
+            return n, i - lo
+    raise ValueError("index outside the groups")
+
+
+def tile_attention_pa_kernel(tc, x_words, x_scales, w_qkv_words, w_qkv_scales, out_0, out_1, out_2):
+    nc = tc.nc
+    q_out = out_0.rearrange("t h d -> t (h d)")
+    k_out = out_1.rearrange("t h d -> t (h d)")
+    v_out = out_2.rearrange("t h d -> t (h d)")
+
+    with ExitStack() as ctx:
+        ctx.enter_context(tc.manual_schedule())
+        keep = ctx.enter_context(tc.tile_pool(name="keep", bufs=1))
+        work = ctx.enter_context(tc.tile_pool(name="work", bufs=2))
+        psum = ctx.enter_context(tc.psum_pool(name="psum", bufs=8))
+
+        w_codes = [keep.tile([P, PASSES, 1024], U8, name="w_codes%d" % b, align_bytes=64) for b in range(NB)]
+        w_planes = [keep.tile([P, PASSES, 512 * (hi - lo)], U8, name="w_planes%d" % n, align_bytes=64)
+                    for n, (lo, hi) in enumerate(W_SCALE_GROUPS)]
+        x_codes = [keep.tile([P, PASSES, 256 * (hi - lo)], U8, name="x_codes%d" % n, align_bytes=64)
+                   for n, (lo, hi) in enumerate(X_CODE_GROUPS)]
+        x_planes = [keep.tile([P, PASSES, P * (hi - lo)], U8, name="x_planes%d" % n, align_bytes=64)
+                    for n, (lo, hi) in enumerate(X_SCALE_GROUPS)]
+
+        warm_in = keep.tile([P, 1], F32, name="warm_in")
+        warm_out = keep.tile([P, 1], F32, name="warm_out")
+        pos = keep.tile([P, N_TILES], F32, name="pos")
+        freq = keep.tile([P, HALF], F32, name="freq")
+        idle_in = keep.tile([P, 512], BF16, name="idle_in")
+
+        nc.gpsimd.memset(idle_in[:], 0.0)
+        nc.vector.memset(warm_in[:], 0.0)
+        nc.vector.memset(freq[:, 0:1], 1.0)
+        nc.scalar.activation(out=warm_out[:], in_=warm_in[:], func=ACT.Sin)
+        nc.vector.memset(w_planes[0][:].bitcast(I32), 0)
+        nc.vector.memset(x_planes[0][:].bitcast(I32), 0)
+        nc.vector.memset(w_planes[1][:].bitcast(I32), 0)
+        nc.vector.memset(w_planes[2][:].bitcast(I32), 0)
+        nc.gpsimd.iota(pos[:], pattern=[[P, N_TILES]], base=0, channel_multiplier=1,
+                       allow_small_or_imprecise_dtypes=True)
+
+        def load_scales(planes, scales, lo, hi):
+            for quad in range(4):
+                nc.sync.dma_start(
+                    out=planes[32 * quad:32 * quad + 4, :, :].bitcast(I32),
+                    in_=scales[:, 4 * quad:4 * quad + 4, lo:hi].rearrange("g r n -> r g n").bitcast(I32),
+                )
+
+        def load_codes(codes, words, lo, hi):
+            nc.sync.dma_start(out=codes[:].bitcast(I32),
+                              in_=words[:, :, lo:hi].rearrange("g p n -> p g n").bitcast(I32))
+
+        def load_w_scales(n):
+            lo, hi = W_SCALE_GROUPS[n]
+            load_scales(w_planes[n], w_qkv_scales, 512 * lo, 512 * hi)
+
+        def load_x_scales(n):
+            lo, hi = X_SCALE_GROUPS[n]
+            load_scales(x_planes[n], x_scales, P * lo, P * hi)
+
+        def load_w_codes(b):
+            load_codes(w_codes[b], w_qkv_words, 1024 * b, 1024 * (b + 1))
+
+        def load_x_codes(n):
+            lo, hi = X_CODE_GROUPS[n]
+            load_codes(x_codes[n], x_words, 256 * lo, 256 * hi)
+
+        load_x_codes(0)
+        load_w_codes(V_BLOCK)
+        load_w_scales(0)
+        load_x_scales(0)
+        load_x_codes(1)
+        load_w_scales(1)
+        load_w_codes(0)
+        load_w_codes(1)
+        load_w_scales(2)
+        load_w_codes(2)
+        load_w_codes(3)
+        load_w_codes(4)
+        load_x_codes(2)
+
+        for j in range(6):
+            n = 2 ** j
+            nc.scalar.activation(out=freq[:, n:2 * n], in_=freq[:, 0:n], func=ACT.Copy,
+                                 scale=THETA ** (-n / float(HALF)))
+
+        angle = keep.tile([P, N_TILES, HALF], F32, name="angle")
+        turns = work.tile([P, N_TILES, HALF], I32, name="turns", tag="prod", bufs=3)
+
+        def reduce_angles(lo, hi):
+            a = angle[:, lo:hi, :]
+            k = turns[:, lo:hi, :]
+            nc.vector.tensor_tensor(out=a, in0=pos[:, lo:hi].unsqueeze(2).to_broadcast([P, hi - lo, HALF]),
+                                    in1=freq[:].unsqueeze(1).to_broadcast([P, hi - lo, HALF]), op=ALU.mult)
+            nc.vector.tensor_scalar(out=k, in0=a, scalar1=1.0 / (2.0 * math.pi), scalar2=None, op0=ALU.mult)
+            nc.vector.scalar_tensor_tensor(out=a, in0=k, scalar=-TWO_PI_HI, in1=a, op0=ALU.mult, op1=ALU.add)
+            nc.vector.scalar_tensor_tensor(out=a, in0=k, scalar=-TWO_PI_LO, in1=a, op0=ALU.mult, op1=ALU.add)
+
+        chain = {}
+
+        def fold(grp):
+            c = {}
+            chain[grp] = c
+            w = work.tile([P, GROUP, 2, 2, HALF], F32, name="fold1", tag="fold1")
+            for a in range(2):
+                for two in range(2):
+                    nc.scalar.activation(out=w[:, :, a, two, :], in_=angle[:, GROUP * grp:GROUP * (grp + 1), :],
+                                         func=ACT.Abs, bias=-(a + two) * math.pi / 2.0, scale=1.0)
+            z = work.tile([P, GROUP, 2, 2 * HALF], F32, name="fold2", tag="fold2")
+            nc.scalar.activation(out=z[:].rearrange("p j a (i w) -> p (j a) i w", w=2),
+                                 in_=w[:].rearrange("p j a w i -> p (j a) i w"), func=ACT.Abs,
+                                 bias=-math.pi, scale=1.0)
+            c["z"] = z
+
+        tables = {}
+
+        def table(t):
+            z = chain[t // GROUP]["z"]
+            tab = work.tile([P, 2, HEADS_PER_BLOCK, 2 * HALF], F32, name="tab", tag="tab", bufs=6)
+            nc.scalar.activation(
+                out=tab[:],
+                in_=z[:, t % GROUP, :, :].unsqueeze(2).to_broadcast([P, 2, HEADS_PER_BLOCK, 2 * HALF]),
+                func=ACT.Sin, bias=-math.pi / 2.0, scale=1.0)
+            tables[t] = tab
+
+        def multiply(t, b):
+            acc = psum.tile([P, 512], F32, name="acc", tag="acc")
+            cn, ci = find_group(X_CODE_GROUPS, t)
+            sn, si = find_group(X_SCALE_GROUPS, t)
+            wn, wi = find_group(W_SCALE_GROUPS, b)
+            for g in range(PASSES):
+                nc.tensor.matmul_mx(
+                    out=acc[:],
+                    lhsT=x_codes[cn][:, g, 256 * ci:256 * (ci + 1)].bitcast(FP4X4),
+                    lhsT_scale=x_planes[sn][:, g, P * si:P * (si + 1)],
+                    rhs=w_codes[b][:, g, :].bitcast(FP4X4),
+                    rhs_scale=w_planes[wn][:, g, 512 * wi:512 * (wi + 1)],
+                    start=(g == 0), stop=(g == PASSES - 1),
+                )
+            return acc
+
+        def v_finish(t, acc, queue):
+            vo = work.tile([P, 512], F32, name="vo", tag="vo", bufs=4)
+            nc.scalar.copy(out=vo[:], in_=acc[:])
+            queue.dma_start(out=v_out[P * t:P * (t + 1), :], in_=vo[:])
+
+        def v_unit(t):
+            v_finish(t, multiply(t, V_BLOCK), nc.scalar)
+
+        def rope_unit(t, b, prod, slot):
+            acc = multiply(t, b)
+            nc.vector.tensor_tensor(
+                out=prod[:, slot, :].rearrange("p (a m w) -> p a m w", a=2, w=2),
+                in0=acc[:].rearrange("p (m a) -> p a m", a=2).unsqueeze(3).to_broadcast([P, 2, 256, 2]),
+                in1=tables[t][:].rearrange("p a h (i w) -> p a (h i) w", w=2),
+                op=ALU.mult)
+
+        def new_job():
+            prod = work.tile([P, ROPE_BLOCKS, 1024], F32, name="prod", tag="prod", bufs=3)
+            rot = work.tile([P, ROPE_BLOCKS, 512], F32, name="rot", tag="rot", bufs=3)
+            return prod, rot
+
+        def combine(engine, prod, rot, lo, hi):
+            engine.tensor_tensor(out=rot[:, lo:hi, :], in0=prod[:, lo:hi, 0:512], in1=prod[:, lo:hi, 512:1024],
+                                 op=ALU.subtract)
+
+        def store_blocks(t, rot, b_lo, b_hi):
+            rows = slice(P * t, P * (t + 1))
+            q_hi = min(b_hi, 4)
+            if b_lo < q_hi:
+                nc.sync.dma_start(out=q_out[rows, 512 * b_lo:512 * q_hi],
+                                  in_=rot[:, b_lo:q_hi, :].rearrange("p u c -> p (u c)"))
+            if b_hi == ROPE_BLOCKS:
+                nc.sync.dma_start(out=k_out[rows, :], in_=rot[:, 4, :])
+
+        idle_out = psum.tile([P, 512], F32, name="acc", tag="acc")
+        for n in range(WARM_MATMULS):
+            nc.tensor.matmul(out=idle_out[:], lhsT=idle_in[:, 0:P], rhs=idle_in[:], start=True, stop=True)
+
+        head_v = [multiply(t, V_BLOCK) for t in range(HEAD_TILES)]
+        reduce_angles(0, HEAD_TILES)
+        reduce_angles(HEAD_TILES, N_TILES)
+        fold(0)
+        for t in range(HEAD_TILES):
+            table(t)
+            if t < 2:
+                v_finish(2 * t, head_v[2 * t], nc.sync)
+                v_finish(2 * t + 1, head_v[2 * t + 1], nc.sync)
+        fold(1)
+        table(4)
+        table(5)
+
+        for b in range(ROPE_BLOCKS):
+            prod, rot = new_job()
+            for t in range(HEAD_TILES):
+                rope_unit(t, b, prod, t)
+            combine(nc.gpsimd, prod, rot, 0, HEAD_TILES)
+            for t in range(HEAD_TILES):
+                rows = slice(P * t, P * (t + 1))
+                if b < 4:
+                    nc.sync.dma_start(out=q_out[rows, 512 * b:512 * (b + 1)], in_=rot[:, t, :])
+                else:
+                    nc.sync.dma_start(out=k_out[rows, :], in_=rot[:, t, :])
+            if b == 0:
+                nc.gpsimd.memset(x_planes[1][:].bitcast(F32), 0.0)
+                load_x_scales(1)
+                load_x_codes(3)
+                load_x_codes(4)
+                load_x_codes(5)
+
+        for t in range(HEAD_TILES, N_TILES - 1):
+            if t + 2 < N_TILES:
+                table(t + 2)
+            nxt = t // GROUP + 1
+            if t % GROUP == 1 and nxt * GROUP < N_TILES:
+                fold(nxt)
+            prod, rot = new_job()
+            for b in range(ROPE_BLOCKS):
+                rope_unit(t, b, prod, b)
+                if b == 2 and t < N_TILES - DEFER_V:
+                    v_unit(t)
+            for lo, hi in (((0, 5),) if t < N_TILES - 2 else ((0, 3), (3, 5))):
+                combine(nc.gpsimd, prod, rot, lo, hi)
+                store_blocks(t, rot, lo, hi)
+
+        t = N_TILES - 1
+        prod, rot = new_job()
+        for b in range(ROPE_BLOCKS):
+            rope_unit(t, b, prod, b)
+        late_v = list(range(N_TILES - DEFER_V, N_TILES))
+        v_unit(late_v[0])
+        v_unit(late_v[1])
+        for n, (lo, hi) in enumerate(((0, 2), (2, 4), (4, 5))):
+            combine(nc.vector, prod, rot, lo, hi)
+            store_blocks(t, rot, lo, hi)
+            v_unit(late_v[2 + n])
+        for tv in late_v[5:]:
+            v_unit(tv)

@@ -165,18 +165,18 @@ def tile_attention_pa_kernel(tc, x_words, x_scales, w_qkv_words, w_qkv_scales, o
                 func=ACT.Sin, bias=-math.pi / 2.0, scale=1.0)
             tables[t] = tab
 
-        def multiply(t, b):
+        def multiply(t, b, lo=0, width=512):
             acc = psum.tile([P, 512], F32, name="acc", tag="acc")
             cn, ci = find_group(X_CODE_GROUPS, t)
             sn, si = find_group(X_SCALE_GROUPS, t)
             wn, wi = find_group(W_SCALE_GROUPS, b)
             for g in range(PASSES):
                 nc.tensor.matmul_mx(
-                    out=acc[:],
+                    out=acc[:, 0:width],
                     lhsT=x_codes[cn][:, g, 256 * ci:256 * (ci + 1)].bitcast(FP4X4),
                     lhsT_scale=x_planes[sn][:, g, P * si:P * (si + 1)],
-                    rhs=w_codes[b][:, g, :].bitcast(FP4X4),
-                    rhs_scale=w_planes[wn][:, g, 512 * wi:512 * (wi + 1)],
+                    rhs=w_codes[b][:, g, 2 * lo:2 * (lo + width)].bitcast(FP4X4),
+                    rhs_scale=w_planes[wn][:, g, 512 * wi + lo:512 * wi + lo + width],
                     start=(g == 0), stop=(g == PASSES - 1),
                 )
             return acc
@@ -270,11 +270,22 @@ def tile_attention_pa_kernel(tc, x_words, x_scales, w_qkv_words, w_qkv_scales, o
         for b in range(ROPE_BLOCKS):
             rope_unit(t, b, prod, b)
         late_v = list(range(N_TILES - DEFER_V, N_TILES))
-        v_unit(late_v[0])
-        v_unit(late_v[1])
+
+        late_vo = work.tile([P, DEFER_V, 512], F32, name="late_vo", tag="prod", bufs=3)
+
+        def late_v_unit(tv, lo=0, width=512):
+            acc = multiply(tv, V_BLOCK, lo, width)
+            vo = late_vo[:, tv - late_v[0], lo:lo + width]
+            nc.scalar.copy(out=vo, in_=acc[:, 0:width])
+            nc.sync.dma_start(out=v_out[P * tv:P * (tv + 1), lo:lo + width], in_=vo)
+
+        late_v_unit(late_v[0])
+        late_v_unit(late_v[1])
         for n, (lo, hi) in enumerate(((0, 2), (2, 4), (4, 5))):
             combine(nc.vector, prod, rot, lo, hi)
             store_blocks(t, rot, lo, hi)
-            v_unit(late_v[2 + n])
-        for tv in late_v[5:]:
-            v_unit(tv)
+            late_v_unit(late_v[2 + n])
+        for tv in late_v[5:-1]:
+            late_v_unit(tv)
+        late_v_unit(late_v[-1], 0, 256)
+        late_v_unit(late_v[-1], 256, 256)

@@ -26,7 +26,7 @@ HALF = D // 2
 HEADS_PER_BLOCK = 512 // D
 GROUP = 4
 HEAD_TILES = 4
-DEFER_V = 8
+DEFER_V = 12
 WARM_MATMULS = 12
 
 W_SCALE_GROUPS = ((5, 6), (0, 2), (2, 5))
@@ -271,11 +271,13 @@ def tile_attention_pa_kernel(tc, x_words, x_scales, w_qkv_words, w_qkv_scales, o
             rope_unit(t, b, prod, b)
         late_v = list(range(N_TILES - DEFER_V, N_TILES))
 
-        late_vo = work.tile([P, DEFER_V, 512], F32, name="late_vo", tag="prod", bufs=3)
+        late_vo = [work.tile([P, min(10, DEFER_V - n), 512], F32, name="late_vo", tag="prod", bufs=3)
+                   for n in range(0, DEFER_V, 10)]
 
         def late_v_unit(tv, lo=0, width=512):
             acc = multiply(tv, V_BLOCK, lo, width)
-            vo = late_vo[:, tv - late_v[0], lo:lo + width]
+            n = tv - late_v[0]
+            vo = late_vo[n // 10][:, n % 10, lo:lo + width]
             nc.scalar.copy(out=vo, in_=acc[:, 0:width])
             nc.sync.dma_start(out=v_out[P * tv:P * (tv + 1), lo:lo + width], in_=vo)
 

@@ -56,12 +56,12 @@ def tile_attention_pa_kernel(tc, x_words, x_scales, w_qkv_words, w_qkv_scales, o
         work = ctx.enter_context(tc.tile_pool(name="work", bufs=2))
         psum = ctx.enter_context(tc.psum_pool(name="psum", bufs=8))
 
-        w_codes = [keep.tile([P, PASSES, 1024], U8, name="w_codes%d" % b, align_bytes=64) for b in range(NB)]
-        w_planes = [keep.tile([P, PASSES, 512 * (hi - lo)], U8, name="w_planes%d" % n, align_bytes=64)
+        w_codes = [keep.tile([P, PASSES, 1024], U8, name="w_codes%d" % b, align_bytes=256) for b in range(NB)]
+        w_planes = [keep.tile([P, PASSES, 512 * (hi - lo)], U8, name="w_planes%d" % n, align_bytes=256)
                     for n, (lo, hi) in enumerate(W_SCALE_GROUPS)]
-        x_codes = [keep.tile([P, PASSES, 256 * (hi - lo)], U8, name="x_codes%d" % n, align_bytes=64)
+        x_codes = [keep.tile([P, PASSES, 256 * (hi - lo)], U8, name="x_codes%d" % n, align_bytes=256)
                    for n, (lo, hi) in enumerate(X_CODE_GROUPS)]
-        x_planes = [keep.tile([P, PASSES, P * (hi - lo)], U8, name="x_planes%d" % n, align_bytes=64)
+        x_planes = [keep.tile([P, PASSES, P * (hi - lo)], U8, name="x_planes%d" % n, align_bytes=256)
                     for n, (lo, hi) in enumerate(X_SCALE_GROUPS)]
 
         warm_in = keep.tile([P, 1], F32, name="warm_in")

@@ -27,7 +27,7 @@ HEADS_PER_BLOCK = 512 // D
 GROUP = 4
 HEAD_TILES = 4
 DEFER_V = 12
-WARM_MATMULS = 12
+WARM_MATMULS = 18
 
 W_SCALE_GROUPS = ((5, 6), (0, 2), (2, 5))
 X_SCALE_GROUPS = ((0, 8), (8, 32))

@@ -27,7 +27,7 @@ HEADS_PER_BLOCK = 512 // D
 GROUP = 4
 HEAD_TILES = 4
 DEFER_V = 12
-WARM_MATMULS = 18
+WARM_MATMULS = 14
 
 W_SCALE_GROUPS = ((5, 6), (0, 2), (2, 5))
 X_SCALE_GROUPS = ((0, 8), (8, 32))
@@ -187,7 +187,7 @@ def tile_attention_pa_kernel(tc, x_words, x_scales, w_qkv_words, w_qkv_scales, o
             queue.dma_start(out=v_out[P * t:P * (t + 1), :], in_=vo[:])
 
         def v_unit(t):
-            v_finish(t, multiply(t, V_BLOCK), nc.scalar)
+            v_finish(t, multiply(t, V_BLOCK), nc.sync)
 
         def rope_unit(t, b, prod, slot):
             acc = multiply(t, b)

@@ -30,7 +30,7 @@ DEFER_V = 12
 WARM_MATMULS = 14
 
 W_SCALE_GROUPS = ((5, 6), (0, 2), (2, 5))
-X_SCALE_GROUPS = ((0, 8), (8, 32))
+X_SCALE_GROUPS = ((0, 4), (4, 8), (8, 32))
 X_CODE_GROUPS = ((0, 2), (2, 4), (4, 8), (8, 16), (16, 24), (24, 32))
 
 TWO_PI_HI = 6.28125
@@ -61,8 +61,9 @@ def tile_attention_pa_kernel(tc, x_words, x_scales, w_qkv_words, w_qkv_scales, o
                     for n, (lo, hi) in enumerate(W_SCALE_GROUPS)]
         x_codes = [keep.tile([P, PASSES, 256 * (hi - lo)], U8, name="x_codes%d" % n, align_bytes=256)
                    for n, (lo, hi) in enumerate(X_CODE_GROUPS)]
-        x_planes = [keep.tile([P, PASSES, P * (hi - lo)], U8, name="x_planes%d" % n, align_bytes=256)
-                    for n, (lo, hi) in enumerate(X_SCALE_GROUPS)]
+        x_planes_head = keep.tile([P, 2, PASSES, 4 * P], U8, name="x_planes_head", align_bytes=256)
+        x_planes_rest = keep.tile([P, PASSES, 24 * P], U8, name="x_planes_rest", align_bytes=256)
+        x_planes = [x_planes_head[:, 0, :, :], x_planes_head[:, 1, :, :], x_planes_rest[:]]
 
         warm_in = keep.tile([P, 1], F32, name="warm_in")
         warm_out = keep.tile([P, 1], F32, name="warm_out")
@@ -75,14 +76,14 @@ def tile_attention_pa_kernel(tc, x_words, x_scales, w_qkv_words, w_qkv_scales, o
         nc.vector.memset(freq[:, 0:1], 1.0)
         nc.scalar.activation(out=warm_out[:], in_=warm_in[:], func=ACT.Sin)
         nc.vector.memset(w_planes[0][:].bitcast(I32), 0)
-        nc.vector.memset(x_planes[0][:].bitcast(I32), 0)
+        nc.vector.memset(x_planes_head[:].bitcast(I32), 0)
         nc.vector.memset(w_planes[1][:].bitcast(I32), 0)
         nc.vector.memset(w_planes[2][:].bitcast(I32), 0)
         nc.gpsimd.iota(pos[:], pattern=[[P, N_TILES]], base=0, channel_multiplier=1,
                        allow_small_or_imprecise_dtypes=True)
 
-        def load_scales(planes, scales, lo, hi):
-            for quad in range(4):
+        def load_scales(planes, scales, lo, hi, quads=(0, 1, 2, 3)):
+            for quad in quads:
                 nc.sync.dma_start(
                     out=planes[32 * quad:32 * quad + 4, :, :].bitcast(I32),
                     in_=scales[:, 4 * quad:4 * quad + 4, lo:hi].rearrange("g r n -> r g n").bitcast(I32),
@@ -92,9 +93,9 @@ def tile_attention_pa_kernel(tc, x_words, x_scales, w_qkv_words, w_qkv_scales, o
             nc.sync.dma_start(out=codes[:].bitcast(I32),
                               in_=words[:, :, lo:hi].rearrange("g p n -> p g n").bitcast(I32))
 
-        def load_w_scales(n):
+        def load_w_scales(n, quads=(0, 1, 2, 3)):
             lo, hi = W_SCALE_GROUPS[n]
-            load_scales(w_planes[n], w_qkv_scales, 512 * lo, 512 * hi)
+            load_scales(w_planes[n], w_qkv_scales, 512 * lo, 512 * hi, quads)
 
         def load_x_scales(n):
             lo, hi = X_SCALE_GROUPS[n]
@@ -108,8 +109,9 @@ def tile_attention_pa_kernel(tc, x_words, x_scales, w_qkv_words, w_qkv_scales, o
             load_codes(x_codes[n], x_words, 256 * lo, 256 * hi)
 
         load_x_codes(0)
+        load_w_scales(0, (0,))
         load_w_codes(V_BLOCK)
-        load_w_scales(0)
+        load_w_scales(0, (1, 2, 3))
         load_x_scales(0)
         load_x_codes(1)
         load_w_scales(1)
@@ -120,6 +122,7 @@ def tile_attention_pa_kernel(tc, x_words, x_scales, w_qkv_words, w_qkv_scales, o
         load_w_codes(3)
         load_w_codes(4)
         load_x_codes(2)
+        load_x_scales(1)
 
         for j in range(6):
             n = 2 ** j
@@ -244,8 +247,8 @@ def tile_attention_pa_kernel(tc, x_words, x_scales, w_qkv_words, w_qkv_scales, o
                 else:
                     nc.sync.dma_start(out=k_out[rows, :], in_=rot[:, t, :])
             if b == 0:
-                nc.gpsimd.memset(x_planes[1][:].bitcast(F32), 0.0)
-                load_x_scales(1)
+                nc.gpsimd.memset(x_planes_rest[:].bitcast(F32), 0.0)
+                load_x_scales(2)
                 load_x_codes(3)
                 load_x_codes(4)
                 load_x_codes(5)

@@ -26,7 +26,7 @@ HALF = D // 2
 HEADS_PER_BLOCK = 512 // D
 GROUP = 4
 HEAD_TILES = 4
-DEFER_V = 12
+DEFER_V = 16
 WARM_MATMULS = 14
 
 W_SCALE_GROUPS = ((5, 6), (0, 2), (2, 5))
@@ -89,6 +89,13 @@ def tile_attention_pa_kernel(tc, x_words, x_scales, w_qkv_words, w_qkv_scales, o
                     in_=scales[:, 4 * quad:4 * quad + 4, lo:hi].rearrange("g r n -> r g n").bitcast(I32),
                 )
 
+        def load_scales_by_row(planes, scales, lo, hi, rows):
+            for r in rows:
+                nc.sync.dma_start(
+                    out=planes[r:P:32, :, :].bitcast(I32),
+                    in_=scales[:, r:16:4, lo:hi].rearrange("g q n -> q g n").bitcast(I32),
+                )
+
         def load_codes(codes, words, lo, hi):
             nc.sync.dma_start(out=codes[:].bitcast(I32),
                               in_=words[:, :, lo:hi].rearrange("g p n -> p g n").bitcast(I32))
@@ -109,10 +116,10 @@ def tile_attention_pa_kernel(tc, x_words, x_scales, w_qkv_words, w_qkv_scales, o
             load_codes(x_codes[n], x_words, 256 * lo, 256 * hi)
 
         load_x_codes(0)
-        load_w_scales(0, (0,))
+        load_scales_by_row(w_planes[0], w_qkv_scales, 512 * V_BLOCK, 512 * (V_BLOCK + 1), (0,))
         load_w_codes(V_BLOCK)
-        load_w_scales(0, (1, 2, 3))
-        load_x_scales(0)
+        load_scales_by_row(w_planes[0], w_qkv_scales, 512 * V_BLOCK, 512 * (V_BLOCK + 1), (1, 2, 3))
+        load_scales_by_row(x_planes[0], x_scales, 0, P * HEAD_TILES, (0, 1, 2, 3))
         load_x_codes(1)
         load_w_scales(1)
         load_w_codes(0)

@@ -27,7 +27,7 @@ HEADS_PER_BLOCK = 512 // D
 GROUP = 4
 HEAD_TILES = 4
 DEFER_V = 16
-WARM_MATMULS = 14
+WARM_MATMULS = 11
 
 W_SCALE_GROUPS = ((5, 6), (0, 2), (2, 5))
 X_SCALE_GROUPS = ((0, 4), (4, 8), (8, 32))
@@ -82,14 +82,7 @@ def tile_attention_pa_kernel(tc, x_words, x_scales, w_qkv_words, w_qkv_scales, o
         nc.gpsimd.iota(pos[:], pattern=[[P, N_TILES]], base=0, channel_multiplier=1,
                        allow_small_or_imprecise_dtypes=True)
 
-        def load_scales(planes, scales, lo, hi, quads=(0, 1, 2, 3)):
-            for quad in quads:
-                nc.sync.dma_start(
-                    out=planes[32 * quad:32 * quad + 4, :, :].bitcast(I32),
-                    in_=scales[:, 4 * quad:4 * quad + 4, lo:hi].rearrange("g r n -> r g n").bitcast(I32),
-                )
-
-        def load_scales_by_row(planes, scales, lo, hi, rows):
+        def load_scales(planes, scales, lo, hi, rows=(0, 1, 2, 3)):
             for r in rows:
                 nc.sync.dma_start(
                     out=planes[r:P:32, :, :].bitcast(I32),
@@ -100,9 +93,9 @@ def tile_attention_pa_kernel(tc, x_words, x_scales, w_qkv_words, w_qkv_scales, o
             nc.sync.dma_start(out=codes[:].bitcast(I32),
                               in_=words[:, :, lo:hi].rearrange("g p n -> p g n").bitcast(I32))
 
-        def load_w_scales(n, quads=(0, 1, 2, 3)):
+        def load_w_scales(n, rows=(0, 1, 2, 3)):
             lo, hi = W_SCALE_GROUPS[n]
-            load_scales(w_planes[n], w_qkv_scales, 512 * lo, 512 * hi, quads)
+            load_scales(w_planes[n], w_qkv_scales, 512 * lo, 512 * hi, rows)
 
         def load_x_scales(n):
             lo, hi = X_SCALE_GROUPS[n]
@@ -116,10 +109,10 @@ def tile_attention_pa_kernel(tc, x_words, x_scales, w_qkv_words, w_qkv_scales, o
             load_codes(x_codes[n], x_words, 256 * lo, 256 * hi)
 
         load_x_codes(0)
-        load_scales_by_row(w_planes[0], w_qkv_scales, 512 * V_BLOCK, 512 * (V_BLOCK + 1), (0,))
+        load_w_scales(0, (0,))
         load_w_codes(V_BLOCK)
-        load_scales_by_row(w_planes[0], w_qkv_scales, 512 * V_BLOCK, 512 * (V_BLOCK + 1), (1, 2, 3))
-        load_scales_by_row(x_planes[0], x_scales, 0, P * HEAD_TILES, (0, 1, 2, 3))
+        load_w_scales(0, (1, 2, 3))
+        load_x_scales(0)
         load_x_codes(1)
         load_w_scales(1)
         load_w_codes(0)

@@ -26,7 +26,7 @@ HALF = D // 2
 HEADS_PER_BLOCK = 512 // D
 GROUP = 4
 HEAD_TILES = 4
-DEFER_V = 16
+DEFER_V = 20
 WARM_MATMULS = 11
 
 W_SCALE_GROUPS = ((5, 6), (0, 2), (2, 5))

@@ -130,7 +130,7 @@ def tile_attention_pa_kernel(tc, x_words, x_scales, w_qkv_words, w_qkv_scales, o
                                  scale=THETA ** (-n / float(HALF)))
 
         angle = keep.tile([P, N_TILES, HALF], F32, name="angle")
-        turns = work.tile([P, N_TILES, HALF], I32, name="turns", tag="prod", bufs=3)
+        turns = work.tile([P, N_TILES, HALF], I32, name="turns", tag="prod", bufs=3, align_bytes=256)
 
         def reduce_angles(lo, hi):
             a = angle[:, lo:hi, :]
@@ -185,7 +185,7 @@ def tile_attention_pa_kernel(tc, x_words, x_scales, w_qkv_words, w_qkv_scales, o
             return acc
 
         def v_finish(t, acc, queue):
-            vo = work.tile([P, 512], F32, name="vo", tag="vo", bufs=4)
+            vo = work.tile([P, 512], F32, name="vo", tag="vo", bufs=4, align_bytes=256)
             nc.scalar.copy(out=vo[:], in_=acc[:])
             queue.dma_start(out=v_out[P * t:P * (t + 1), :], in_=vo[:])
 
@@ -201,8 +201,8 @@ def tile_attention_pa_kernel(tc, x_words, x_scales, w_qkv_words, w_qkv_scales, o
                 op=ALU.mult)
 
         def new_job():
-            prod = work.tile([P, ROPE_BLOCKS, 1024], F32, name="prod", tag="prod", bufs=3)
-            rot = work.tile([P, ROPE_BLOCKS, 512], F32, name="rot", tag="rot", bufs=3)
+            prod = work.tile([P, ROPE_BLOCKS, 1024], F32, name="prod", tag="prod", bufs=3, align_bytes=256)
+            rot = work.tile([P, ROPE_BLOCKS, 512], F32, name="rot", tag="rot", bufs=3, align_bytes=256)
             return prod, rot
 
         def combine(engine, prod, rot, lo, hi):
@@ -274,7 +274,7 @@ def tile_attention_pa_kernel(tc, x_words, x_scales, w_qkv_words, w_qkv_scales, o
             rope_unit(t, b, prod, b)
         late_v = list(range(N_TILES - DEFER_V, N_TILES))
 
-        late_vo = [work.tile([P, min(10, DEFER_V - n), 512], F32, name="late_vo", tag="prod", bufs=3)
+        late_vo = [work.tile([P, min(10, DEFER_V - n), 512], F32, name="late_vo", tag="prod", bufs=3, align_bytes=256)
                    for n in range(0, DEFER_V, 10)]
 
         def late_v_unit(tv, lo=0, width=512):

@@ -27,6 +27,7 @@ HEADS_PER_BLOCK = 512 // D
 GROUP = 4
 HEAD_TILES = 4
 DEFER_V = 20
+FINE_TILES = 3
 WARM_MATMULS = 11
 
 W_SCALE_GROUPS = ((5, 6), (0, 2), (2, 5))
@@ -264,7 +265,7 @@ def tile_attention_pa_kernel(tc, x_words, x_scales, w_qkv_words, w_qkv_scales, o
                 rope_unit(t, b, prod, b)
                 if b == 2 and t < N_TILES - DEFER_V:
                     v_unit(t)
-            for lo, hi in (((0, 5),) if t < N_TILES - 2 else ((0, 3), (3, 5))):
+            for lo, hi in (((0, 5),) if t < N_TILES - 1 - FINE_TILES else ((0, 2), (2, 4), (4, 5))):
                 combine(nc.gpsimd, prod, rot, lo, hi)
                 store_blocks(t, rot, lo, hi)
 

@@ -26,6 +26,7 @@ HALF = D // 2
 HEADS_PER_BLOCK = 512 // D
 GROUP = 4
 HEAD_TILES = 4
+LOOP_V_TILES = (4, 7, 11, 14, 18, 21, 25, 28)
 DEFER_V = 20
 FINE_TILES = 3
 WARM_MATMULS = 11
@@ -263,7 +264,7 @@ def tile_attention_pa_kernel(tc, x_words, x_scales, w_qkv_words, w_qkv_scales, o
             prod, rot = new_job()
             for b in range(ROPE_BLOCKS):
                 rope_unit(t, b, prod, b)
-                if b == 2 and t < N_TILES - DEFER_V:
+                if b == 2 and t in LOOP_V_TILES:
                     v_unit(t)
             for lo, hi in (((0, 5),) if t < N_TILES - 1 - FINE_TILES else ((0, 2), (2, 4), (4, 5))):
                 combine(nc.gpsimd, prod, rot, lo, hi)
@@ -273,14 +274,15 @@ def tile_attention_pa_kernel(tc, x_words, x_scales, w_qkv_words, w_qkv_scales, o
         prod, rot = new_job()
         for b in range(ROPE_BLOCKS):
             rope_unit(t, b, prod, b)
-        late_v = list(range(N_TILES - DEFER_V, N_TILES))
+        late_v = [tv for tv in range(HEAD_TILES, N_TILES) if tv not in LOOP_V_TILES]
+        assert len(late_v) == DEFER_V
 
         late_vo = [work.tile([P, min(10, DEFER_V - n), 512], F32, name="late_vo", tag="prod", bufs=3, align_bytes=256)
                    for n in range(0, DEFER_V, 10)]
 
         def late_v_unit(tv, lo=0, width=512):
             acc = multiply(tv, V_BLOCK, lo, width)
-            n = tv - late_v[0]
+            n = late_v.index(tv)
             vo = late_vo[n // 10][:, n % 10, lo:lo + width]
             nc.scalar.copy(out=vo, in_=acc[:, 0:width])
             nc.sync.dma_start(out=v_out[P * tv:P * (tv + 1), lo:lo + width], in_=vo)

@@ -29,7 +29,7 @@ HEAD_TILES = 4
 LOOP_V_TILES = (4, 7, 11, 14, 18, 21, 25, 28)
 DEFER_V = 20
 FINE_TILES = 3
-WARM_MATMULS = 11
+WARM_MATMULS = 9
 
 W_SCALE_GROUPS = ((5, 6), (0, 2), (2, 5))
 X_SCALE_GROUPS = ((0, 4), (4, 8), (8, 32))
@@ -73,12 +73,13 @@ def tile_attention_pa_kernel(tc, x_words, x_scales, w_qkv_words, w_qkv_scales, o
         freq = keep.tile([P, HALF], F32, name="freq")
         idle_in = keep.tile([P, 512], BF16, name="idle_in")
 
+        nc.gpsimd.memset(w_planes[0][:].bitcast(F32), 0.0)
         nc.gpsimd.memset(idle_in[:], 0.0)
+        nc.vector.memset(x_planes[0].bitcast(I32), 0)
         nc.vector.memset(warm_in[:], 0.0)
         nc.vector.memset(freq[:, 0:1], 1.0)
         nc.scalar.activation(out=warm_out[:], in_=warm_in[:], func=ACT.Sin)
-        nc.vector.memset(w_planes[0][:].bitcast(I32), 0)
-        nc.vector.memset(x_planes_head[:].bitcast(I32), 0)
+        nc.vector.memset(x_planes[1].bitcast(I32), 0)
         nc.vector.memset(w_planes[1][:].bitcast(I32), 0)
         nc.vector.memset(w_planes[2][:].bitcast(I32), 0)
         nc.gpsimd.iota(pos[:], pattern=[[P, N_TILES]], base=0, channel_multiplier=1,

@@ -32,7 +32,7 @@ FINE_TILES = 3
 WARM_MATMULS = 9
 
 W_SCALE_GROUPS = ((5, 6), (0, 2), (2, 5))
-X_SCALE_GROUPS = ((0, 4), (4, 8), (8, 32))
+X_SCALE_GROUPS = ((0, 2), (2, 4), (4, 8), (8, 32))
 X_CODE_GROUPS = ((0, 2), (2, 4), (4, 8), (8, 16), (16, 24), (24, 32))
 
 TWO_PI_HI = 6.28125
@@ -63,9 +63,11 @@ def tile_attention_pa_kernel(tc, x_words, x_scales, w_qkv_words, w_qkv_scales, o
                     for n, (lo, hi) in enumerate(W_SCALE_GROUPS)]
         x_codes = [keep.tile([P, PASSES, 256 * (hi - lo)], U8, name="x_codes%d" % n, align_bytes=256)
                    for n, (lo, hi) in enumerate(X_CODE_GROUPS)]
-        x_planes_head = keep.tile([P, 2, PASSES, 4 * P], U8, name="x_planes_head", align_bytes=256)
+        x_planes_first = keep.tile([P, PASSES, 2 * P], U8, name="x_planes_first", align_bytes=256)
+        x_planes_head = keep.tile([P, PASSES, 2 * P], U8, name="x_planes_head", align_bytes=256)
+        x_planes_next = keep.tile([P, PASSES, 4 * P], U8, name="x_planes_next", align_bytes=256)
         x_planes_rest = keep.tile([P, PASSES, 24 * P], U8, name="x_planes_rest", align_bytes=256)
-        x_planes = [x_planes_head[:, 0, :, :], x_planes_head[:, 1, :, :], x_planes_rest[:]]
+        x_planes = [x_planes_first[:], x_planes_head[:], x_planes_next[:], x_planes_rest[:]]
 
         warm_in = keep.tile([P, 1], F32, name="warm_in")
         warm_out = keep.tile([P, 1], F32, name="warm_out")
@@ -73,13 +75,14 @@ def tile_attention_pa_kernel(tc, x_words, x_scales, w_qkv_words, w_qkv_scales, o
         freq = keep.tile([P, HALF], F32, name="freq")
         idle_in = keep.tile([P, 512], BF16, name="idle_in")
 
-        nc.gpsimd.memset(w_planes[0][:].bitcast(F32), 0.0)
+        nc.gpsimd.memset(x_planes[0].bitcast(F32), 0.0)
         nc.gpsimd.memset(idle_in[:], 0.0)
-        nc.vector.memset(x_planes[0].bitcast(I32), 0)
+        nc.vector.memset(w_planes[0][:].bitcast(I32), 0)
+        nc.vector.memset(x_planes[1].bitcast(I32), 0)
         nc.vector.memset(warm_in[:], 0.0)
         nc.vector.memset(freq[:, 0:1], 1.0)
         nc.scalar.activation(out=warm_out[:], in_=warm_in[:], func=ACT.Sin)
-        nc.vector.memset(x_planes[1].bitcast(I32), 0)
+        nc.vector.memset(x_planes[2].bitcast(I32), 0)
         nc.vector.memset(w_planes[1][:].bitcast(I32), 0)
         nc.vector.memset(w_planes[2][:].bitcast(I32), 0)
         nc.gpsimd.iota(pos[:], pattern=[[P, N_TILES]], base=0, channel_multiplier=1,
@@ -100,9 +103,9 @@ def tile_attention_pa_kernel(tc, x_words, x_scales, w_qkv_words, w_qkv_scales, o
             lo, hi = W_SCALE_GROUPS[n]
             load_scales(w_planes[n], w_qkv_scales, 512 * lo, 512 * hi, rows)
 
-        def load_x_scales(n):
+        def load_x_scales(n, rows=(0, 1, 2, 3)):
             lo, hi = X_SCALE_GROUPS[n]
-            load_scales(x_planes[n], x_scales, P * lo, P * hi)
+            load_scales(x_planes[n], x_scales, P * lo, P * hi, rows)
 
         def load_w_codes(b):
             load_codes(w_codes[b], w_qkv_words, 1024 * b, 1024 * (b + 1))
@@ -112,11 +115,12 @@ def tile_attention_pa_kernel(tc, x_words, x_scales, w_qkv_words, w_qkv_scales, o
             load_codes(x_codes[n], x_words, 256 * lo, 256 * hi)
 
         load_x_codes(0)
-        load_w_scales(0, (0,))
+        load_x_scales(0, (0,))
         load_w_codes(V_BLOCK)
-        load_w_scales(0, (1, 2, 3))
-        load_x_scales(0)
+        load_x_scales(0, (1, 2, 3))
+        load_w_scales(0)
         load_x_codes(1)
+        load_x_scales(1)
         load_w_scales(1)
         load_w_codes(0)
         load_w_codes(1)
@@ -125,7 +129,7 @@ def tile_attention_pa_kernel(tc, x_words, x_scales, w_qkv_words, w_qkv_scales, o
         load_w_codes(3)
         load_w_codes(4)
         load_x_codes(2)
-        load_x_scales(1)
+        load_x_scales(2)
 
         for j in range(6):
             n = 2 ** j
@@ -251,7 +255,7 @@ def tile_attention_pa_kernel(tc, x_words, x_scales, w_qkv_words, w_qkv_scales, o
                     nc.sync.dma_start(out=k_out[rows, :], in_=rot[:, t, :])
             if b == 0:
                 nc.gpsimd.memset(x_planes_rest[:].bitcast(F32), 0.0)
-                load_x_scales(2)
+                load_x_scales(3)
                 load_x_codes(3)
                 load_x_codes(4)
                 load_x_codes(5)

import math
from contextlib import ExitStack

import concourse.mybir as mybir

T, DIM, H, HKV, D = 4096, 2048, 16, 4, 128
THETA = 10000.0
N_OUT = (H + 2 * HKV) * D
FLOPS = 2 * T * DIM * N_OUT

F32 = mybir.dt.float32
I32 = mybir.dt.int32
U8 = mybir.dt.uint8
BF16 = mybir.dt.bfloat16
FP4X4 = mybir.dt.float4_e2m1fn_x4
ACT = mybir.ActivationFunctionType
ALU = mybir.AluOpType

P = 128
PASSES = DIM // 512
N_TILES = T // P
NB = N_OUT // 512
ROPE_BLOCKS = 5
V_BLOCK = 5
HALF = D // 2
HEADS_PER_BLOCK = 512 // D
GROUP = 4
HEAD_TILES = 4
LOOP_V_TILES = (4, 7, 11, 14, 18, 21, 25, 28)
DEFER_V = 20
FINE_TILES = 3
WARM_MATMULS = 9

W_SCALE_GROUPS = ((5, 6), (0, 2), (2, 5))
X_SCALE_GROUPS = ((0, 2), (2, 4), (4, 8), (8, 32))
X_CODE_GROUPS = ((0, 2), (2, 4), (4, 8), (8, 16), (16, 24), (24, 32))

TWO_PI_HI = 6.28125
TWO_PI_LO = 2.0 * math.pi - TWO_PI_HI


def find_group(groups, i):
    for n, (lo, hi) in enumerate(groups):
        if lo <= i < hi:
            return n, i - lo
    raise ValueError("index outside the groups")


def tile_attention_pa_kernel(tc, x_words, x_scales, w_qkv_words, w_qkv_scales, out_0, out_1, out_2):
    nc = tc.nc
    q_out = out_0.rearrange("t h d -> t (h d)")
    k_out = out_1.rearrange("t h d -> t (h d)")
    v_out = out_2.rearrange("t h d -> t (h d)")

    with ExitStack() as ctx:
        ctx.enter_context(tc.manual_schedule())
        keep = ctx.enter_context(tc.tile_pool(name="keep", bufs=1))
        work = ctx.enter_context(tc.tile_pool(name="work", bufs=2))
        psum = ctx.enter_context(tc.psum_pool(name="psum", bufs=8))

        w_codes = [keep.tile([P, PASSES, 1024], U8, name="w_codes%d" % b, align_bytes=256) for b in range(NB)]
        w_planes = [keep.tile([P, PASSES, 512 * (hi - lo)], U8, name="w_planes%d" % n, align_bytes=256)
                    for n, (lo, hi) in enumerate(W_SCALE_GROUPS)]
        x_codes = [keep.tile([P, PASSES, 256 * (hi - lo)], U8, name="x_codes%d" % n, align_bytes=256)
                   for n, (lo, hi) in enumerate(X_CODE_GROUPS)]
        x_planes_first = keep.tile([P, PASSES, 2 * P], U8, name="x_planes_first", align_bytes=256)
        x_planes_head = keep.tile([P, PASSES, 2 * P], U8, name="x_planes_head", align_bytes=256)
        x_planes_next = keep.tile([P, PASSES, 4 * P], U8, name="x_planes_next", align_bytes=256)
        x_planes_rest = keep.tile([P, PASSES, 24 * P], U8, name="x_planes_rest", align_bytes=256)
        x_planes = [x_planes_first[:], x_planes_head[:], x_planes_next[:], x_planes_rest[:]]

        warm_in = keep.tile([P, 1], F32, name="warm_in")
        warm_out = keep.tile([P, 1], F32, name="warm_out")
        pos = keep.tile([P, N_TILES], F32, name="pos")
        freq = keep.tile([P, HALF], F32, name="freq")
        idle_in = keep.tile([P, 512], BF16, name="idle_in")

        nc.gpsimd.memset(x_planes[0].bitcast(F32), 0.0)
        nc.gpsimd.memset(idle_in[:], 0.0)
        nc.vector.memset(w_planes[0][:].bitcast(I32), 0)
        nc.vector.memset(x_planes[1].bitcast(I32), 0)
        nc.vector.memset(warm_in[:], 0.0)
        nc.vector.memset(freq[:, 0:1], 1.0)
        nc.scalar.activation(out=warm_out[:], in_=warm_in[:], func=ACT.Sin)
        nc.vector.memset(x_planes[2].bitcast(I32), 0)
        nc.vector.memset(w_planes[1][:].bitcast(I32), 0)
        nc.vector.memset(w_planes[2][:].bitcast(I32), 0)
        nc.gpsimd.iota(pos[:], pattern=[[P, N_TILES]], base=0, channel_multiplier=1,
                       allow_small_or_imprecise_dtypes=True)

        def load_scales(planes, scales, lo, hi, rows=(0, 1, 2, 3)):
            for r in rows:
                nc.sync.dma_start(
                    out=planes[r:P:32, :, :].bitcast(I32),
                    in_=scales[:, r:16:4, lo:hi].rearrange("g q n -> q g n").bitcast(I32),
                )

        def load_codes(codes, words, lo, hi):
            nc.sync.dma_start(out=codes[:].bitcast(I32),
                              in_=words[:, :, lo:hi].rearrange("g p n -> p g n").bitcast(I32))

        def load_w_scales(n, rows=(0, 1, 2, 3)):
            lo, hi = W_SCALE_GROUPS[n]
            load_scales(w_planes[n], w_qkv_scales, 512 * lo, 512 * hi, rows)

        def load_x_scales(n, rows=(0, 1, 2, 3)):
            lo, hi = X_SCALE_GROUPS[n]
            load_scales(x_planes[n], x_scales, P * lo, P * hi, rows)

        def load_w_codes(b):
            load_codes(w_codes[b], w_qkv_words, 1024 * b, 1024 * (b + 1))

        def load_x_codes(n):
            lo, hi = X_CODE_GROUPS[n]
            load_codes(x_codes[n], x_words, 256 * lo, 256 * hi)

        load_x_codes(0)
        load_x_scales(0, (0,))
        load_w_codes(V_BLOCK)
        load_x_scales(0, (1, 2, 3))
        load_w_scales(0)
        load_x_codes(1)
        load_x_scales(1)
        load_w_scales(1)
        load_w_codes(0)
        load_w_codes(1)
        load_w_scales(2)
        load_w_codes(2)
        load_w_codes(3)
        load_w_codes(4)
        load_x_codes(2)
        load_x_scales(2)

        for j in range(6):
            n = 2 ** j
            nc.scalar.activation(out=freq[:, n:2 * n], in_=freq[:, 0:n], func=ACT.Copy,
                                 scale=THETA ** (-n / float(HALF)))

        angle = keep.tile([P, N_TILES, HALF], F32, name="angle")
        turns = work.tile([P, N_TILES, HALF], I32, name="turns", tag="prod", bufs=3, align_bytes=256)

        def reduce_angles(lo, hi):
            a = angle[:, lo:hi, :]
            k = turns[:, lo:hi, :]
            nc.vector.tensor_tensor(out=a, in0=pos[:, lo:hi].unsqueeze(2).to_broadcast([P, hi - lo, HALF]),
                                    in1=freq[:].unsqueeze(1).to_broadcast([P, hi - lo, HALF]), op=ALU.mult)
            nc.vector.tensor_scalar(out=k, in0=a, scalar1=1.0 / (2.0 * math.pi), scalar2=None, op0=ALU.mult)
            nc.vector.scalar_tensor_tensor(out=a, in0=k, scalar=-TWO_PI_HI, in1=a, op0=ALU.mult, op1=ALU.add)
            nc.vector.scalar_tensor_tensor(out=a, in0=k, scalar=-TWO_PI_LO, in1=a, op0=ALU.mult, op1=ALU.add)

        chain = {}

        def fold(grp):
            c = {}
            chain[grp] = c
            w = work.tile([P, GROUP, 2, 2, HALF], F32, name="fold1", tag="fold1")
            for a in range(2):
                for two in range(2):
                    nc.scalar.activation(out=w[:, :, a, two, :], in_=angle[:, GROUP * grp:GROUP * (grp + 1), :],
                                         func=ACT.Abs, bias=-(a + two) * math.pi / 2.0, scale=1.0)
            z = work.tile([P, GROUP, 2, 2 * HALF], F32, name="fold2", tag="fold2")
            nc.scalar.activation(out=z[:].rearrange("p j a (i w) -> p (j a) i w", w=2),
                                 in_=w[:].rearrange("p j a w i -> p (j a) i w"), func=ACT.Abs,
                                 bias=-math.pi, scale=1.0)
            c["z"] = z

        tables = {}

        def table(t):
            z = chain[t // GROUP]["z"]
            tab = work.tile([P, 2, HEADS_PER_BLOCK, 2 * HALF], F32, name="tab", tag="tab", bufs=6)
            nc.scalar.activation(
                out=tab[:],
                in_=z[:, t % GROUP, :, :].unsqueeze(2).to_broadcast([P, 2, HEADS_PER_BLOCK, 2 * HALF]),
                func=ACT.Sin, bias=-math.pi / 2.0, scale=1.0)
            tables[t] = tab

        def multiply(t, b, lo=0, width=512):
            acc = psum.tile([P, 512], F32, name="acc", tag="acc")
            cn, ci = find_group(X_CODE_GROUPS, t)
            sn, si = find_group(X_SCALE_GROUPS, t)
            wn, wi = find_group(W_SCALE_GROUPS, b)
            for g in range(PASSES):
                nc.tensor.matmul_mx(
                    out=acc[:, 0:width],
                    lhsT=x_codes[cn][:, g, 256 * ci:256 * (ci + 1)].bitcast(FP4X4),
                    lhsT_scale=x_planes[sn][:, g, P * si:P * (si + 1)],
                    rhs=w_codes[b][:, g, 2 * lo:2 * (lo + width)].bitcast(FP4X4),
                    rhs_scale=w_planes[wn][:, g, 512 * wi + lo:512 * wi + lo + width],
                    start=(g == 0), stop=(g == PASSES - 1),
                )
            return acc

        def v_finish(t, acc, queue):
            vo = work.tile([P, 512], F32, name="vo", tag="vo", bufs=4, align_bytes=256)
            nc.scalar.copy(out=vo[:], in_=acc[:])
            queue.dma_start(out=v_out[P * t:P * (t + 1), :], in_=vo[:])

        def v_unit(t):
            v_finish(t, multiply(t, V_BLOCK), nc.sync)

        def rope_unit(t, b, prod, slot):
            acc = multiply(t, b)
            nc.vector.tensor_tensor(
                out=prod[:, slot, :].rearrange("p (a m w) -> p a m w", a=2, w=2),
                in0=acc[:].rearrange("p (m a) -> p a m", a=2).unsqueeze(3).to_broadcast([P, 2, 256, 2]),
                in1=tables[t][:].rearrange("p a h (i w) -> p a (h i) w", w=2),
                op=ALU.mult)

        def new_job():
            prod = work.tile([P, ROPE_BLOCKS, 1024], F32, name="prod", tag="prod", bufs=3, align_bytes=256)
            rot = work.tile([P, ROPE_BLOCKS, 512], F32, name="rot", tag="rot", bufs=3, align_bytes=256)
            return prod, rot

        def combine(engine, prod, rot, lo, hi):
            engine.tensor_tensor(out=rot[:, lo:hi, :], in0=prod[:, lo:hi, 0:512], in1=prod[:, lo:hi, 512:1024],
                                 op=ALU.subtract)

        def store_blocks(t, rot, b_lo, b_hi):
            rows = slice(P * t, P * (t + 1))
            q_hi = min(b_hi, 4)
            if b_lo < q_hi:
                nc.sync.dma_start(out=q_out[rows, 512 * b_lo:512 * q_hi],
                                  in_=rot[:, b_lo:q_hi, :].rearrange("p u c -> p (u c)"))
            if b_hi == ROPE_BLOCKS:
                nc.sync.dma_start(out=k_out[rows, :], in_=rot[:, 4, :])

        idle_out = psum.tile([P, 512], F32, name="acc", tag="acc")
        for n in range(WARM_MATMULS):
            nc.tensor.matmul(out=idle_out[:], lhsT=idle_in[:, 0:P], rhs=idle_in[:], start=True, stop=True)

        head_v = [multiply(t, V_BLOCK) for t in range(HEAD_TILES)]
        reduce_angles(0, HEAD_TILES)
        reduce_angles(HEAD_TILES, N_TILES)
        fold(0)
        for t in range(HEAD_TILES):
            table(t)
            if t < 2:
                v_finish(2 * t, head_v[2 * t], nc.sync)
                v_finish(2 * t + 1, head_v[2 * t + 1], nc.sync)
        fold(1)
        table(4)
        table(5)

        for b in range(ROPE_BLOCKS):
            prod, rot = new_job()
            for t in range(HEAD_TILES):
                rope_unit(t, b, prod, t)
            combine(nc.gpsimd, prod, rot, 0, HEAD_TILES)
            for t in range(HEAD_TILES):
                rows = slice(P * t, P * (t + 1))
                if b < 4:
                    nc.sync.dma_start(out=q_out[rows, 512 * b:512 * (b + 1)], in_=rot[:, t, :])
                else:
                    nc.sync.dma_start(out=k_out[rows, :], in_=rot[:, t, :])
            if b == 0:
                nc.gpsimd.memset(x_planes_rest[:].bitcast(F32), 0.0)
                load_x_scales(3)
                load_x_codes(3)
                load_x_codes(4)
                load_x_codes(5)

        for t in range(HEAD_TILES, N_TILES - 1):
            if t + 2 < N_TILES:
                table(t + 2)
            nxt = t // GROUP + 1
            if t % GROUP == 1 and nxt * GROUP < N_TILES:
                fold(nxt)
            prod, rot = new_job()
            for b in range(ROPE_BLOCKS):
                rope_unit(t, b, prod, b)
                if b == 2 and t in LOOP_V_TILES:
                    v_unit(t)
            for lo, hi in (((0, 5),) if t < N_TILES - 1 - FINE_TILES else ((0, 2), (2, 4), (4, 5))):
                combine(nc.gpsimd, prod, rot, lo, hi)
                store_blocks(t, rot, lo, hi)

        t = N_TILES - 1
        prod, rot = new_job()
        for b in range(ROPE_BLOCKS):
            rope_unit(t, b, prod, b)
        late_v = [tv for tv in range(HEAD_TILES, N_TILES) if tv not in LOOP_V_TILES]
        assert len(late_v) == DEFER_V

        late_vo = [work.tile([P, min(10, DEFER_V - n), 512], F32, name="late_vo", tag="prod", bufs=3, align_bytes=256)
                   for n in range(0, DEFER_V, 10)]

        def late_v_unit(tv, lo=0, width=512):
            acc = multiply(tv, V_BLOCK, lo, width)
            n = late_v.index(tv)
            vo = late_vo[n // 10][:, n % 10, lo:lo + width]
            nc.scalar.copy(out=vo, in_=acc[:, 0:width])
            nc.sync.dma_start(out=v_out[P * tv:P * (tv + 1), lo:lo + width], in_=vo)

        late_v_unit(late_v[0])
        late_v_unit(late_v[1])
        for n, (lo, hi) in enumerate(((0, 2), (2, 4), (4, 5))):
            combine(nc.vector, prod, rot, lo, hi)
            store_blocks(t, rot, lo, hi)
            late_v_unit(late_v[2 + n])
        for tv in late_v[5:-1]:
            late_v_unit(tv)
        late_v_unit(late_v[-1], 0, 256)
        late_v_unit(late_v[-1], 256, 256)
